import numpy as np
import ml_dtypes


def mxq(x, axis, fmt="e4m3"):
    dtype, down = {"e4m3": (ml_dtypes.float8_e4m3fn, 7), "e5m2": (ml_dtypes.float8_e5m2, 14)}[fmt]
    v = np.moveaxis(np.asarray(x, np.float32).astype(ml_dtypes.bfloat16).astype(np.float64), axis, -1)
    blocks = v.reshape(v.shape[:-1] + (-1, 32))
    amax = np.abs(blocks).max(-1, keepdims=True)
    byte = np.maximum(np.where(amax > 0, np.frexp(amax)[1] - 1 + 127, 0) - down, 1)
    scale = np.exp2(byte - 127.0)
    codes = (blocks / scale).astype(np.float32).astype(dtype).astype(np.float64)
    return np.moveaxis((codes * scale).reshape(v.shape), -1, axis)


WIDE = False


def mx_kscale(k):
    if not WIDE:
        return np.ones(k)
    levels = np.array([10, -10, 5, -5, 0])
    a = np.random.permutation(np.resize(levels, k // 512 * 4)).reshape(k // 512, 4)
    idx = np.arange(k)
    return np.exp2(a[idx // 512, idx % 128 // 32])


BF16 = ml_dtypes.bfloat16


def bf(x):
    return np.asarray(x, np.float32).astype(BF16)


def f64(x):
    return np.asarray(x).astype(np.float64)


B, C, T, E, H = 1, 48, 128, 512, 4
D = E // H
S = C * T


def heads(y):
    return np.moveaxis(y.reshape(B, C, T, H, D), 3, 1)


def setup_inputs():
    s = mx_kscale(E)
    return {"hidden_states": bf(np.random.standard_normal((B, S, E)) * s),
            "wk": bf(np.random.standard_normal((E, E)) * 2.0 / np.sqrt(E) / s[None, :]),
            "bk": bf(np.random.standard_normal(E) * 0.3),
            "wv": bf(np.random.standard_normal((E, E)) * 2.0 / np.sqrt(E) / s[None, :]),
            "bv": bf(np.random.standard_normal(E) * 0.3)}


def reference(hidden_states, wk, bk, wv, bv):
    xq = mxq(f64(hidden_states), 2, "e4m3")
    k = heads((xq @ mxq(f64(wk), 1, "e4m3").T) + f64(bk))
    v = heads((xq @ mxq(f64(wv), 1, "e4m3").T) + f64(bv))
    return k, v, k.mean(axis=3), v.mean(axis=3)

@@ -1,0 +1,277 @@
+from contextlib import ExitStack
+
+import concourse.mybir as mybir
+from concourse.masks import make_identity
+
+FLOPS = 2 * 6144 * 512 * 1024
+
+F32 = mybir.dt.float32
+BF16 = mybir.dt.bfloat16
+U32 = mybir.dt.uint32
+U8 = mybir.dt.uint8
+FP8X4 = mybir.dt.float8_e4m3fn_x4
+ADD = mybir.AluOpType.add
+MULT = mybir.AluOpType.mult
+
+P = 128
+FAMILIES = 3
+SG_BANKS = (0, 3, 6)
+Q_LAG = 4
+R_LAG = 2
+M_PER_Y = 2
+T_AT = {0: (1, 0), 3: (1, 1), 6: (1, 2), 9: (1, 3), 26: (2, 0), 30: (2, 1), 34: (2, 2), 38: (2, 3)}
+
+
+def tile_chunkedattention_pb_t_kernel(
+    tc, hidden_states, wk, bk, wv, bv, out_0, out_1, out_2, out_3
+):
+    nc = tc.nc
+    with ExitStack() as ctx:
+        const = ctx.enter_context(tc.tile_pool(name="const", bufs=1))
+        stage = ctx.enter_context(tc.tile_pool(name="stage", bufs=3))
+        ypool = ctx.enter_context(tc.tile_pool(name="ypool", bufs=6))
+        psum = ctx.enter_context(tc.psum_pool(name="psum", bufs=2))
+        ctx.enter_context(tc.manual_schedule())
+
+        hs = hidden_states.rearrange("b (g p jh i) e -> (b g) p jh i e", p=P, jh=2, i=8)
+        w_dram = [w.rearrange("(ob p) e -> p ob e", p=P) for w in (wk, wv)]
+        b_dram = [b.rearrange("(o n) -> o n", o=1) for b in (bk, bv)]
+        y_dram = [
+            o.rearrange("b h c t d -> (b h) (c t d)").rearrange("h (g p r) -> g p h r", g=FAMILIES, p=P)
+            for o in (out_0, out_1)
+        ]
+        mean_dram = [o.rearrange("b h c d -> (b h c) d") for o in (out_2, out_3)]
+
+        ident_f = const.tile([P, P], F32, name="ident_f")
+        ident_b = const.tile([P, P], BF16, name="ident_b")
+        ones = const.tile([P, P], BF16, name="ones")
+        bias_row = const.tile([P, 1024], BF16, name="bias_row")
+        bias_bc = const.tile([P, 2, 4, P], F32, name="bias_bc")
+        bcol = const.tile([P, 8], F32, name="bcol")
+        w_sb = [const.tile([P, 4, 512], BF16, name="w_sb%d" % kv) for kv in range(2)]
+        w_codes = [const.tile([P, 512], U32, name="w_codes%d" % kv, align_bytes=64) for kv in range(2)]
+        w_scales = [const.tile([P, 512], U8, name="w_scales%d" % kv, align_bytes=64) for kv in range(2)]
+        x_sb = [const.tile([P, 2, 8, 512], BF16, name="x_sb%d" % g) for g in range(FAMILIES)]
+        x_codes = [const.tile([P, 2048], U32, name="x_codes%d" % g, align_bytes=64) for g in range(FAMILIES)]
+        x_scales = [const.tile([P, 2048], U8, name="x_scales%d" % g, align_bytes=64) for g in range(FAMILIES)]
+        red = const.tile([P, 8, 48], F32, name="red")
+        mean_sb = const.tile([P, 8, 48], F32, name="mean_sb")
+        mt_sb = const.tile([P, 3, P], F32, name="mt_sb")
+
+        state = {"clock": 0, "pending": []}
+
+        def later(lag, fn):
+            state["pending"].append((state["clock"] + lag, fn))
+
+        def tick():
+            state["clock"] += 1
+            due = [x for x in state["pending"] if x[0] <= state["clock"]]
+            state["pending"] = [x for x in state["pending"] if x[0] > state["clock"]]
+            for x in due:
+                x[1]()
+
+        nc.vector.memset(bias_row[:], 0.0)
+        nc.vector.memset(ones[:], 1.0)
+        make_identity(nc, ident_f[:])
+        make_identity(nc, ident_b[:])
+        for kv in range(2):
+            nc.scalar.dma_start(out=bias_row[0:1, 512 * kv : 512 * kv + 512], in_=b_dram[kv])
+
+        def load_x(g, a, b):
+            nc.sync.dma_start(out=x_sb[g][:, :, a:b, :], in_=hs[g][:, :, a:b, :])
+
+        nc.sync.dma_start(out=w_sb[0][:], in_=w_dram[0])
+        load_x(0, 0, 2)
+        nc.sync.dma_start(out=w_sb[1][:], in_=w_dram[1])
+        load_x(0, 2, 4)
+        load_x(0, 4, 8)
+        load_x(1, 0, 4)
+        load_x(1, 4, 8)
+        load_x(2, 0, 4)
+        load_x(2, 4, 8)
+
+        for kv in range(2):
+            bb_ps = psum.tile([P, 512], F32, name="bb_ps", tag="m")
+            nc.tensor.matmul(
+                out=bb_ps[:], lhsT=ones[:], rhs=bias_row[:, 512 * kv : 512 * kv + 512], start=True, stop=True
+            )
+            nc.vector.tensor_copy(out=bias_bc[:, kv].rearrange("p h d -> p (h d)"), in_=bb_ps[:])
+
+        def bias_columns():
+            bc_ps = psum.tile([P, 8, P], BF16, name="bc_ps", tag="m")
+            for fb in range(8):
+                nc.tensor.transpose(bc_ps[:, fb, :], bias_row[:, P * fb : P * fb + P], ident_b[:])
+            later(3, lambda: nc.vector.tensor_copy(out=bcol[:], in_=bc_ps[:, :, 0]))
+
+        def transposed_bank(words, tag):
+            bank = psum.tile([P, 2, 2, P], F32, name="bank_" + tag, tag=tag, bufs=(4 if tag == "y" else 2))
+            for s in range(2):
+                for u in range(2):
+                    nc.tensor.transpose(bank[:, s, u, :], words[s][:, P * u : P * u + P], ident_f[:])
+            return bank
+
+        def regroup(engine_copy, grouped, b, bank):
+            view = grouped[:].bitcast(F32).rearrange("q (s t u) -> q s t u", s=4, u=2)
+            engine_copy(out=view[:, 2 * b : 2 * b + 2], in_=bank[:].rearrange("q s u t -> q s t u"))
+
+        def prepare_w(kv):
+            words = w_sb[kv][:].bitcast(F32)
+            grouped = stage.tile([P, 2048], BF16, name="grouped", align_bytes=64)
+            banks = [transposed_bank([words[:, 2 * b + s, :] for s in range(2)], "y") for b in range(2)]
+            regroup(nc.vector.tensor_copy, grouped, 0, banks[0])
+            regroup(nc.scalar.copy, grouped, 1, banks[1])
+            nc.vector.quantize_mx(out=w_codes[kv][:].bitcast(FP8X4), scales=w_scales[kv][:], in_=grouped[:])
+
+        def prepare_x(g, rr, lag, share):
+            words = x_sb[g][:].bitcast(F32)
+            grouped = stage.tile([P, 2048], BF16, name="grouped", align_bytes=64)
+            banks = [transposed_bank([words[:, jh, 2 * rr + b, :] for jh in range(2)], "t") for b in range(2)]
+            regroup(nc.scalar.copy, grouped, 0, banks[0])
+            regroup(nc.vector.tensor_copy if share else nc.scalar.copy, grouped, 1, banks[1])
+            cols = slice(512 * rr, 512 * rr + 512)
+
+            def quantise():
+                nc.vector.quantize_mx(
+                    out=x_codes[g][:, cols].bitcast(FP8X4), scales=x_scales[g][:, cols], in_=grouped[:]
+                )
+
+            later(lag, quantise)
+
+        units = {}
+
+        def y_bank(g, kv, hh, i):
+            key = (g, kv, hh)
+            if key not in units:
+                units[key] = ypool.tile([P, 2, 2, 8, P], F32, name="yb")
+            yb = units[key]
+            y_ps = psum.tile([P, 2, 256], F32, name="y_ps", tag="y", bufs=4)
+            feats = slice(256 * hh, 256 * hh + 256)
+            for jh in range(2):
+                toks = slice(P * (2 * i + jh), P * (2 * i + jh) + P)
+                nc.tensor.matmul_mx(
+                    out=y_ps[:, jh, :],
+                    lhsT=x_codes[g][:, toks].bitcast(FP8X4),
+                    lhsT_scale=x_scales[g][:, toks],
+                    rhs=w_codes[kv][:, feats].bitcast(FP8X4),
+                    rhs_scale=w_scales[kv][:, feats],
+                    start=True,
+                    stop=True,
+                )
+            dst = yb[:, :, :, i, :].rearrange("p h jh d -> p jh h d")
+            src = y_ps[:].rearrange("p jh (h d) -> p jh h d", h=2)
+            bias = bias_bc[:, kv, 2 * hh : 2 * hh + 2, :].unsqueeze(1).to_broadcast([P, 2, 2, P])
+            if i in SG_BANKS:
+                nc.scalar.copy(out=dst, in_=src)
+                nc.gpsimd.tensor_tensor(out=dst, in0=dst, in1=bias, op=ADD)
+            else:
+                nc.vector.tensor_tensor(out=dst, in0=src, in1=bias, op=ADD)
+
+        def store_unit(g, kv, hh):
+            yb = units[(g, kv, hh)]
+            nc.sync.dma_start(
+                out=y_dram[kv][g][:, 2 * hh : 2 * hh + 2, :], in_=yb[:].rearrange("p h jh i d -> p h (jh i d)")
+            )
+
+        m_tiles = {}
+
+        def m_pass(g, fb, i):
+            kv, h = fb // 4, fb % 4
+            if i == 0:
+                m_tiles[(g, fb)] = psum.tile([P, 256], F32, name="m_ps", tag="m")
+            m_ps = m_tiles[(g, fb)]
+            feats = slice(P * h, P * h + P)
+            toks = slice(256 * i, 256 * i + 256)
+            nc.tensor.matmul_mx(
+                out=m_ps[:],
+                lhsT=w_codes[kv][:, feats].bitcast(FP8X4),
+                lhsT_scale=w_scales[kv][:, feats],
+                rhs=x_codes[g][:, toks].bitcast(FP8X4),
+                rhs_scale=x_scales[g][:, toks],
+                start=(i == 0),
+                stop=(i == 7),
+            )
+            if i == 7:
+
+                def reduce_block():
+                    nc.vector.tensor_reduce(
+                        out=red[:, fb, 16 * g : 16 * g + 16],
+                        in_=m_ps[:].rearrange("d (jh c s) -> d c jh s", jh=2, s=8),
+                        axis=mybir.AxisListType.XY,
+                        op=ADD,
+                    )
+                    if g == FAMILIES - 1:
+                        nc.vector.tensor_scalar(
+                            out=mean_sb[:, fb, :],
+                            in0=red[:, fb, :],
+                            scalar1=1.0 / 128.0,
+                            scalar2=bcol[:, fb : fb + 1],
+                            op0=MULT,
+                            op1=ADD,
+                        )
+
+                later(R_LAG, reduce_block)
+
+        prepare_w(0)
+        tick()
+        prepare_x(0, 0, 1, True)
+        tick()
+        prepare_w(1)
+        tick()
+        prepare_x(0, 1, 4, False)
+        tick()
+        bias_columns()
+        tick()
+
+        def k_banks(rr):
+            for i in (2 * rr, 2 * rr + 1):
+                for hh in range(2):
+                    y_bank(0, 0, hh, i)
+                    tick()
+
+        k_banks(0)
+        prepare_x(0, 2, 4, False)
+        tick()
+        prepare_x(0, 3, 6, False)
+        tick()
+        k_banks(1)
+        k_banks(2)
+        k_banks(3)
+        store_unit(0, 0, 0)
+        store_unit(0, 0, 1)
+
+        y_list = [
+            (g, kv, hh, i)
+            for g in range(FAMILIES)
+            for kv in range(2)
+            for hh in range(2)
+            for i in range(8)
+            if (g, kv) != (0, 0)
+        ]
+        m_list = [(g, fb, i) for g in range(FAMILIES) for fb in range(8) for i in range(8)]
+        m_next = 0
+        for n, (g, kv, hh, i) in enumerate(y_list):
+            if n in T_AT:
+                prepare_x(T_AT[n][0], T_AT[n][1], Q_LAG, False)
+                tick()
+            y_bank(g, kv, hh, i)
+            for m in m_list[m_next : m_next + M_PER_Y]:
+                m_pass(m[0], m[1], m[2])
+            m_next += M_PER_Y
+            tick()
+            if i == 7:
+                store_unit(g, kv, hh)
+        for m in m_list[m_next:]:
+            m_pass(m[0], m[1], m[2])
+            tick()
+        for n in range(8):
+            tick()
+
+        mt_ps = psum.tile([P, 3, P], F32, name="mt_ps", tag="t")
+        flat = mean_sb[:].rearrange("d fb c -> d (fb c)")
+        for b in range(3):
+            nc.tensor.transpose(mt_ps[:, b, :], flat[:, P * b : P * b + P], ident_f[:])
+        nc.vector.tensor_copy(out=mt_sb[:], in_=mt_ps[:])
+        nc.sync.dma_start(out=mean_dram[0][0:128, :], in_=mt_sb[:, 0, :])
+        nc.sync.dma_start(out=mean_dram[0][128:192, :], in_=mt_sb[0:64, 1, :])
+        nc.sync.dma_start(out=mean_dram[1][0:64, :], in_=mt_sb[64:128, 1, :])
+        nc.sync.dma_start(out=mean_dram[1][64:192, :], in_=mt_sb[:, 2, :])

@@ -16,10 +16,11 @@ MULT = mybir.AluOpType.mult
 P = 128
 FAMILIES = 3
 SG_BANKS = (0, 3, 6)
+SG_BANKS_FIRST = (0, 2, 4, 6)
 Q_LAG = 4
 R_LAG = 2
 M_PER_Y = 2
-T_AT = {0: (1, 0), 3: (1, 1), 6: (1, 2), 9: (1, 3), 26: (2, 0), 30: (2, 1), 34: (2, 2), 38: (2, 3)}
+T_AT = {2: (1, 1), 5: (1, 2), 8: (1, 3), 26: (2, 0), 30: (2, 1), 34: (2, 2), 38: (2, 3)}
 
 
 def tile_chunkedattention_pb_t_kernel(
@@ -45,6 +46,7 @@ def tile_chunkedattention_pb_t_kernel(
         ident_f = const.tile([P, P], F32, name="ident_f")
         ident_b = const.tile([P, P], BF16, name="ident_b")
         ones = const.tile([P, P], BF16, name="ones")
+        bias_in = const.tile([1, 1024], BF16, name="bias_in")
         bias_row = const.tile([P, 1024], BF16, name="bias_row")
         bias_bc = const.tile([P, 2, 4, P], F32, name="bias_bc")
         bcol = const.tile([P, 8], F32, name="bcol")
@@ -70,38 +72,40 @@ def tile_chunkedattention_pb_t_kernel(
             for x in due:
                 x[1]()
 
+        for kv in range(2):
+            nc.scalar.dma_start(out=bias_in[0:1, 512 * kv : 512 * kv + 512], in_=b_dram[kv])
         nc.vector.memset(bias_row[:], 0.0)
         nc.vector.memset(ones[:], 1.0)
         make_identity(nc, ident_f[:])
         make_identity(nc, ident_b[:])
-        for kv in range(2):
-            nc.scalar.dma_start(out=bias_row[0:1, 512 * kv : 512 * kv + 512], in_=b_dram[kv])
 
         def load_x(g, a, b):
             nc.sync.dma_start(out=x_sb[g][:, :, a:b, :], in_=hs[g][:, :, a:b, :])
 
         nc.sync.dma_start(out=w_sb[0][:], in_=w_dram[0])
         load_x(0, 0, 2)
-        nc.sync.dma_start(out=w_sb[1][:], in_=w_dram[1])
         load_x(0, 2, 4)
         load_x(0, 4, 8)
+        nc.sync.dma_start(out=w_sb[1][:], in_=w_dram[1])
         load_x(1, 0, 4)
         load_x(1, 4, 8)
         load_x(2, 0, 4)
         load_x(2, 4, 8)
 
-        for kv in range(2):
-            bb_ps = psum.tile([P, 512], F32, name="bb_ps", tag="m")
+        def bias_everywhere(kv, tag, lag):
+            bb_ps = psum.tile([P, 512], F32, name="bb_ps", tag=tag, bufs=(4 if tag == "y" else 2))
             nc.tensor.matmul(
                 out=bb_ps[:], lhsT=ones[:], rhs=bias_row[:, 512 * kv : 512 * kv + 512], start=True, stop=True
             )
-            nc.vector.tensor_copy(out=bias_bc[:, kv].rearrange("p h d -> p (h d)"), in_=bb_ps[:])
+            later(
+                lag, lambda: nc.vector.tensor_copy(out=bias_bc[:, kv].rearrange("p h d -> p (h d)"), in_=bb_ps[:])
+            )
 
         def bias_columns():
-            bc_ps = psum.tile([P, 8, P], BF16, name="bc_ps", tag="m")
+            bc_ps = psum.tile([P, 8, P], BF16, name="bc_ps", tag="y", bufs=4)
             for fb in range(8):
                 nc.tensor.transpose(bc_ps[:, fb, :], bias_row[:, P * fb : P * fb + P], ident_b[:])
-            later(3, lambda: nc.vector.tensor_copy(out=bcol[:], in_=bc_ps[:, :, 0]))
+            later(2, lambda: nc.vector.tensor_copy(out=bcol[:], in_=bc_ps[:, :, 0]))
 
         def transposed_bank(words, tag):
             bank = psum.tile([P, 2, 2, P], F32, name="bank_" + tag, tag=tag, bufs=(4 if tag == "y" else 2))
@@ -114,13 +118,20 @@ def tile_chunkedattention_pb_t_kernel(
             view = grouped[:].bitcast(F32).rearrange("q (s t u) -> q s t u", s=4, u=2)
             engine_copy(out=view[:, 2 * b : 2 * b + 2], in_=bank[:].rearrange("q s u t -> q s t u"))
 
-        def prepare_w(kv):
+        def prepare_w(kv, lag):
             words = w_sb[kv][:].bitcast(F32)
             grouped = stage.tile([P, 2048], BF16, name="grouped", align_bytes=64)
             banks = [transposed_bank([words[:, 2 * b + s, :] for s in range(2)], "y") for b in range(2)]
             regroup(nc.vector.tensor_copy, grouped, 0, banks[0])
             regroup(nc.scalar.copy, grouped, 1, banks[1])
-            nc.vector.quantize_mx(out=w_codes[kv][:].bitcast(FP8X4), scales=w_scales[kv][:], in_=grouped[:])
+            if kv == 0:
+                nc.vector.tensor_copy(out=bias_row[0:1, :], in_=bias_in[:])
+            later(
+                lag,
+                lambda: nc.vector.quantize_mx(
+                    out=w_codes[kv][:].bitcast(FP8X4), scales=w_scales[kv][:], in_=grouped[:]
+                ),
+            )
 
         def prepare_x(g, rr, lag, share):
             words = x_sb[g][:].bitcast(F32)
@@ -160,7 +171,7 @@ def tile_chunkedattention_pb_t_kernel(
             dst = yb[:, :, :, i, :].rearrange("p h jh d -> p jh h d")
             src = y_ps[:].rearrange("p jh (h d) -> p jh h d", h=2)
             bias = bias_bc[:, kv, 2 * hh : 2 * hh + 2, :].unsqueeze(1).to_broadcast([P, 2, 2, P])
-            if i in SG_BANKS:
+            if i in (SG_BANKS_FIRST if key[:2] == (0, 0) else SG_BANKS):
                 nc.scalar.copy(out=dst, in_=src)
                 nc.gpsimd.tensor_tensor(out=dst, in0=dst, in1=bias, op=ADD)
             else:
@@ -171,6 +182,14 @@ def tile_chunkedattention_pb_t_kernel(
             nc.sync.dma_start(
                 out=y_dram[kv][g][:, 2 * hh : 2 * hh + 2, :], in_=yb[:].rearrange("p h jh i d -> p h (jh i d)")
             )
+
+        def store_piece(g, kv, hh, a, b):
+            yb = units[(g, kv, hh)]
+            for h in range(2):
+                nc.sync.dma_start(
+                    out=y_dram[kv][g][:, 2 * hh + h, :].rearrange("p (jh i d) -> p jh i d", jh=2, i=8)[:, :, a:b, :],
+                    in_=yb[:, h, :, a:b, :],
+                )
 
         m_tiles = {}
 
@@ -211,32 +230,54 @@ def tile_chunkedattention_pb_t_kernel(
 
                 later(R_LAG, reduce_block)
 
-        prepare_w(0)
+        def finish_means():
+            mt_ps = psum.tile([P, 3, P], F32, name="mt_ps", tag="t")
+            flat = mean_sb[:].rearrange("d fb c -> d (fb c)")
+            for b in range(3):
+                nc.tensor.transpose(mt_ps[:, b, :], flat[:, P * b : P * b + P], ident_f[:])
+            nc.scalar.copy(out=mt_sb[:], in_=mt_ps[:])
+            nc.sync.dma_start(out=mean_dram[0][0:128, :], in_=mt_sb[:, 0, :])
+            nc.sync.dma_start(out=mean_dram[0][128:192, :], in_=mt_sb[0:64, 1, :])
+            nc.sync.dma_start(out=mean_dram[1][0:64, :], in_=mt_sb[64:128, 1, :])
+            nc.sync.dma_start(out=mean_dram[1][64:192, :], in_=mt_sb[:, 2, :])
+
+        def first_work(rr):
+            for i in (2 * rr, 2 * rr + 1):
+                y_bank(0, 0, 0, i)
+                m_pass(0, 0, i)
+                m_pass(0, 1, i)
+                tick()
+
+        def second_unit(a, b):
+            for i in range(a, b):
+                y_bank(0, 0, 1, i)
+                tick()
+
+        prepare_w(0, 1)
         tick()
         prepare_x(0, 0, 1, True)
+        bias_everywhere(0, "m", 1)
         tick()
-        prepare_w(1)
+        prepare_x(0, 1, 2, False)
         tick()
-        prepare_x(0, 1, 4, False)
+        first_work(0)
+        prepare_x(0, 2, 3, False)
         tick()
+        first_work(1)
+        prepare_x(0, 3, 4, False)
+        tick()
+        second_unit(0, 4)
+        first_work(2)
+        first_work(3)
+        store_unit(0, 0, 0)
+        prepare_w(1, 3)
+        bias_everywhere(1, "y", 2)
         bias_columns()
         tick()
-
-        def k_banks(rr):
-            for i in (2 * rr, 2 * rr + 1):
-                for hh in range(2):
-                    y_bank(0, 0, hh, i)
-                    tick()
-
-        k_banks(0)
-        prepare_x(0, 2, 4, False)
+        second_unit(4, 6)
+        prepare_x(1, 0, Q_LAG, False)
         tick()
-        prepare_x(0, 3, 6, False)
-        tick()
-        k_banks(1)
-        k_banks(2)
-        k_banks(3)
-        store_unit(0, 0, 0)
+        second_unit(6, 8)
         store_unit(0, 0, 1)
 
         y_list = [
@@ -247,7 +288,7 @@ def tile_chunkedattention_pb_t_kernel(
             for i in range(8)
             if (g, kv) != (0, 0)
         ]
-        m_list = [(g, fb, i) for g in range(FAMILIES) for fb in range(8) for i in range(8)]
+        m_list = [(g, fb, i) for g in range(FAMILIES) for fb in range(8) for i in range(8) if (g, fb) not in ((0, 0), (0, 1))]
         m_next = 0
         for n, (g, kv, hh, i) in enumerate(y_list):
             if n in T_AT:
@@ -265,13 +306,4 @@ def tile_chunkedattention_pb_t_kernel(
             tick()
         for n in range(8):
             tick()
-
-        mt_ps = psum.tile([P, 3, P], F32, name="mt_ps", tag="t")
-        flat = mean_sb[:].rearrange("d fb c -> d (fb c)")
-        for b in range(3):
-            nc.tensor.transpose(mt_ps[:, b, :], flat[:, P * b : P * b + P], ident_f[:])
-        nc.vector.tensor_copy(out=mt_sb[:], in_=mt_ps[:])
-        nc.sync.dma_start(out=mean_dram[0][0:128, :], in_=mt_sb[:, 0, :])
-        nc.sync.dma_start(out=mean_dram[0][128:192, :], in_=mt_sb[0:64, 1, :])
-        nc.sync.dma_start(out=mean_dram[1][0:64, :], in_=mt_sb[64:128, 1, :])
-        nc.sync.dma_start(out=mean_dram[1][64:192, :], in_=mt_sb[:, 2, :])
+        finish_means()

@@ -15,7 +15,7 @@ MULT = mybir.AluOpType.mult
 
 P = 128
 FAMILIES = 3
-SG_BANKS = (0, 3, 6)
+SG_BANKS = (0, 2, 4, 6)
 SG_BANKS_FIRST = (0, 2, 4, 6)
 Q_LAG = 4
 R_LAG = 2

@@ -15,8 +15,8 @@ MULT = mybir.AluOpType.mult
 
 P = 128
 FAMILIES = 3
-SG_BANKS = (0, 2, 4, 6)
-SG_BANKS_FIRST = (0, 2, 4, 6)
+SG_BANKS = (1, 5)
+SG_BANKS_FIRST = (1, 5)
 Q_LAG = 4
 R_LAG = 2
 M_PER_Y = 2

@@ -16,10 +16,11 @@ MULT = mybir.AluOpType.mult
 P = 128
 FAMILIES = 3
 SG_BANKS = (1, 5)
-SG_BANKS_FIRST = (1, 5)
+SG_OF_UNIT = ((), (), (), (), (), (), (), (), (), (), (), ())
 Q_LAG = 4
 R_LAG = 2
-M_PER_Y = 2
+M_START = 8
+M_END = 76
 T_AT = {2: (1, 1), 5: (1, 2), 8: (1, 3), 26: (2, 0), 30: (2, 1), 34: (2, 2), 38: (2, 3)}
 
 
@@ -54,8 +55,16 @@ def tile_chunkedattention_pb_t_kernel(
         w_codes = [const.tile([P, 512], U32, name="w_codes%d" % kv, align_bytes=64) for kv in range(2)]
         w_scales = [const.tile([P, 512], U8, name="w_scales%d" % kv, align_bytes=64) for kv in range(2)]
         x_sb = [const.tile([P, 2, 8, 512], BF16, name="x_sb%d" % g) for g in range(FAMILIES)]
-        x_codes = [const.tile([P, 2048], U32, name="x_codes%d" % g, align_bytes=64) for g in range(FAMILIES)]
-        x_scales = [const.tile([P, 2048], U8, name="x_scales%d" % g, align_bytes=64) for g in range(FAMILIES)]
+        x_codes2 = const.tile([P, 16, P], U32, name="x_codes2", align_bytes=64)
+        x_scales2 = const.tile([P, 16, P], U8, name="x_scales2", align_bytes=64)
+        x_codes01 = const.tile([P, 16, 2, P], U32, name="x_codes01", align_bytes=64)
+        x_scales01 = const.tile([P, 16, 2, P], U8, name="x_scales01", align_bytes=64)
+
+        def token_set(g, s):
+            if g == 2:
+                return x_codes2[:, s, :], x_scales2[:, s, :]
+            return x_codes01[:, s, g, :], x_scales01[:, s, g, :]
+
         red = const.tile([P, 8, 48], F32, name="red")
         mean_sb = const.tile([P, 8, 48], F32, name="mean_sb")
         mt_sb = const.tile([P, 3, P], F32, name="mt_sb")
@@ -97,9 +106,8 @@ def tile_chunkedattention_pb_t_kernel(
             nc.tensor.matmul(
                 out=bb_ps[:], lhsT=ones[:], rhs=bias_row[:, 512 * kv : 512 * kv + 512], start=True, stop=True
             )
-            later(
-                lag, lambda: nc.vector.tensor_copy(out=bias_bc[:, kv].rearrange("p h d -> p (h d)"), in_=bb_ps[:])
-            )
+            copy_out = nc.vector.tensor_copy if kv == 0 else nc.scalar.copy
+            later(lag, lambda: copy_out(out=bias_bc[:, kv].rearrange("p h d -> p (h d)"), in_=bb_ps[:]))
 
         def bias_columns():
             bc_ps = psum.tile([P, 8, P], BF16, name="bc_ps", tag="y", bufs=4)
@@ -122,7 +130,7 @@ def tile_chunkedattention_pb_t_kernel(
             words = w_sb[kv][:].bitcast(F32)
             grouped = stage.tile([P, 2048], BF16, name="grouped", align_bytes=64)
             banks = [transposed_bank([words[:, 2 * b + s, :] for s in range(2)], "y") for b in range(2)]
-            regroup(nc.vector.tensor_copy, grouped, 0, banks[0])
+            regroup(nc.vector.tensor_copy if kv == 0 else nc.scalar.copy, grouped, 0, banks[0])
             regroup(nc.scalar.copy, grouped, 1, banks[1])
             if kv == 0:
                 nc.vector.tensor_copy(out=bias_row[0:1, :], in_=bias_in[:])
@@ -139,12 +147,21 @@ def tile_chunkedattention_pb_t_kernel(
             banks = [transposed_bank([words[:, jh, 2 * rr + b, :] for jh in range(2)], "t") for b in range(2)]
             regroup(nc.scalar.copy, grouped, 0, banks[0])
             regroup(nc.vector.tensor_copy if share else nc.scalar.copy, grouped, 1, banks[1])
-            cols = slice(512 * rr, 512 * rr + 512)
 
             def quantise():
-                nc.vector.quantize_mx(
-                    out=x_codes[g][:, cols].bitcast(FP8X4), scales=x_scales[g][:, cols], in_=grouped[:]
-                )
+                if g == 2:
+                    sets = slice(4 * rr, 4 * rr + 4)
+                    nc.vector.quantize_mx(
+                        out=x_codes2[:, sets, :].rearrange("q s t -> q (s t)").bitcast(FP8X4),
+                        scales=x_scales2[:, sets, :].rearrange("q s t -> q (s t)"),
+                        in_=grouped[:],
+                    )
+                else:
+                    for s in range(4):
+                        codes, scales = token_set(g, 4 * rr + s)
+                        nc.vector.quantize_mx(
+                            out=codes.bitcast(FP8X4), scales=scales, in_=grouped[:, 512 * s : 512 * s + 512]
+                        )
 
             later(lag, quantise)
 
@@ -158,11 +175,11 @@ def tile_chunkedattention_pb_t_kernel(
             y_ps = psum.tile([P, 2, 256], F32, name="y_ps", tag="y", bufs=4)
             feats = slice(256 * hh, 256 * hh + 256)
             for jh in range(2):
-                toks = slice(P * (2 * i + jh), P * (2 * i + jh) + P)
+                codes, scales = token_set(g, 2 * i + jh)
                 nc.tensor.matmul_mx(
                     out=y_ps[:, jh, :],
-                    lhsT=x_codes[g][:, toks].bitcast(FP8X4),
-                    lhsT_scale=x_scales[g][:, toks],
+                    lhsT=codes.bitcast(FP8X4),
+                    lhsT_scale=scales,
                     rhs=w_codes[kv][:, feats].bitcast(FP8X4),
                     rhs_scale=w_scales[kv][:, feats],
                     start=True,
@@ -171,7 +188,7 @@ def tile_chunkedattention_pb_t_kernel(
             dst = yb[:, :, :, i, :].rearrange("p h jh d -> p jh h d")
             src = y_ps[:].rearrange("p jh (h d) -> p jh h d", h=2)
             bias = bias_bc[:, kv, 2 * hh : 2 * hh + 2, :].unsqueeze(1).to_broadcast([P, 2, 2, P])
-            if i in (SG_BANKS_FIRST if key[:2] == (0, 0) else SG_BANKS):
+            if i in SG_OF_UNIT[4 * g + 2 * kv + hh]:
                 nc.scalar.copy(out=dst, in_=src)
                 nc.gpsimd.tensor_tensor(out=dst, in0=dst, in1=bias, op=ADD)
             else:
@@ -195,37 +212,49 @@ def tile_chunkedattention_pb_t_kernel(
 
         def m_pass(g, fb, i):
             kv, h = fb // 4, fb % 4
+            last = 7 if g == 2 else 15
             if i == 0:
                 m_tiles[(g, fb)] = psum.tile([P, 256], F32, name="m_ps", tag="m")
             m_ps = m_tiles[(g, fb)]
             feats = slice(P * h, P * h + P)
-            toks = slice(256 * i, 256 * i + 256)
+            if g == 2:
+                codes = x_codes2[:, 2 * i : 2 * i + 2, :].rearrange("q s t -> q (s t)")
+                scales = x_scales2[:, 2 * i : 2 * i + 2, :].rearrange("q s t -> q (s t)")
+            else:
+                codes = x_codes01[:, i, :, :].rearrange("q g t -> q (g t)")
+                scales = x_scales01[:, i, :, :].rearrange("q g t -> q (g t)")
             nc.tensor.matmul_mx(
                 out=m_ps[:],
                 lhsT=w_codes[kv][:, feats].bitcast(FP8X4),
                 lhsT_scale=w_scales[kv][:, feats],
-                rhs=x_codes[g][:, toks].bitcast(FP8X4),
-                rhs_scale=x_scales[g][:, toks],
+                rhs=codes.bitcast(FP8X4),
+                rhs_scale=scales,
                 start=(i == 0),
-                stop=(i == 7),
+                stop=(i == last),
             )
-            if i == 7:
+            if i == last:
 
                 def reduce_block():
-                    nc.vector.tensor_reduce(
-                        out=red[:, fb, 16 * g : 16 * g + 16],
-                        in_=m_ps[:].rearrange("d (jh c s) -> d c jh s", jh=2, s=8),
-                        axis=mybir.AxisListType.XY,
-                        op=ADD,
-                    )
-                    if g == FAMILIES - 1:
-                        nc.vector.tensor_scalar(
+                    if g == 0:
+                        nc.vector.tensor_reduce(
+                            out=red[:, fb, 0:32],
+                            in_=m_ps[:].rearrange("d (c s) -> d c s", s=8),
+                            axis=mybir.AxisListType.X,
+                            op=ADD,
+                        )
+                    else:
+                        nc.vector.tensor_reduce(
+                            out=red[:, fb, 32:48],
+                            in_=m_ps[:].rearrange("d (jh c s) -> d c jh s", jh=2, s=8),
+                            axis=mybir.AxisListType.XY,
+                            op=ADD,
+                        )
+                        nc.scalar.activation(
                             out=mean_sb[:, fb, :],
-                            in0=red[:, fb, :],
-                            scalar1=1.0 / 128.0,
-                            scalar2=bcol[:, fb : fb + 1],
-                            op0=MULT,
-                            op1=ADD,
+                            in_=red[:, fb, :],
+                            func=mybir.ActivationFunctionType.Identity,
+                            bias=bcol[:, fb : fb + 1],
+                            scale=1.0 / 128.0,
                         )
 
                 later(R_LAG, reduce_block)
@@ -244,8 +273,6 @@ def tile_chunkedattention_pb_t_kernel(
         def first_work(rr):
             for i in (2 * rr, 2 * rr + 1):
                 y_bank(0, 0, 0, i)
-                m_pass(0, 0, i)
-                m_pass(0, 1, i)
                 tick()
 
         def second_unit(a, b):
@@ -288,22 +315,22 @@ def tile_chunkedattention_pb_t_kernel(
             for i in range(8)
             if (g, kv) != (0, 0)
         ]
-        m_list = [(g, fb, i) for g in range(FAMILIES) for fb in range(8) for i in range(8) if (g, fb) not in ((0, 0), (0, 1))]
+        m_list = [(0, fb, i) for fb in range(8) for i in range(16)] + [(2, fb, i) for fb in range(8) for i in range(8)]
         m_next = 0
         for n, (g, kv, hh, i) in enumerate(y_list):
             if n in T_AT:
                 prepare_x(T_AT[n][0], T_AT[n][1], Q_LAG, False)
                 tick()
             y_bank(g, kv, hh, i)
-            for m in m_list[m_next : m_next + M_PER_Y]:
+            m_upto = min(192, max(0, 192 * (n + 1 - M_START) // (M_END - M_START)))
+            for m in m_list[m_next:m_upto]:
                 m_pass(m[0], m[1], m[2])
-            m_next += M_PER_Y
+            m_next = m_upto
             tick()
-            if i == 7:
+            if n == M_END + 3:
+                finish_means()
+            if (g, kv, hh) == (2, 1, 1):
+                if i in (3, 5, 7):
+                    store_piece(g, kv, hh, {3: 0, 5: 4, 7: 6}[i], i + 1)
+            elif i == 7:
                 store_unit(g, kv, hh)
-        for m in m_list[m_next:]:
-            m_pass(m[0], m[1], m[2])
-            tick()
-        for n in range(8):
-            tick()
-        finish_means()

@@ -11,17 +11,13 @@ U32 = mybir.dt.uint32
 U8 = mybir.dt.uint8
 FP8X4 = mybir.dt.float8_e4m3fn_x4
 ADD = mybir.AluOpType.add
-MULT = mybir.AluOpType.mult
+AXIS = mybir.AxisListType
+IDENTITY = mybir.ActivationFunctionType.Identity
 
 P = 128
 FAMILIES = 3
-SG_BANKS = (1, 5)
-SG_OF_UNIT = ((), (), (), (), (), (), (), (), (), (), (), ())
-Q_LAG = 4
-R_LAG = 2
-M_START = 8
-M_END = 76
-T_AT = {2: (1, 1), 5: (1, 2), 8: (1, 3), 26: (2, 0), 30: (2, 1), 34: (2, 2), 38: (2, 3)}
+ROUNDS = 24
+DENSE_ROUNDS = range(11, 17)
 
 
 def tile_chunkedattention_pb_t_kernel(
@@ -35,7 +31,7 @@ def tile_chunkedattention_pb_t_kernel(
         psum = ctx.enter_context(tc.psum_pool(name="psum", bufs=2))
         ctx.enter_context(tc.manual_schedule())
 
-        hs = hidden_states.rearrange("b (g p jh i) e -> (b g) p jh i e", p=P, jh=2, i=8)
+        x_dram = hidden_states.rearrange("b (g p jh i) e -> (b g) p jh i e", p=P, jh=2, i=8)
         w_dram = [w.rearrange("(ob p) e -> p ob e", p=P) for w in (wk, wv)]
         b_dram = [b.rearrange("(o n) -> o n", o=1) for b in (bk, bv)]
         y_dram = [
@@ -49,135 +45,99 @@ def tile_chunkedattention_pb_t_kernel(
         ones = const.tile([P, P], BF16, name="ones")
         bias_in = const.tile([1, 1024], BF16, name="bias_in")
         bias_row = const.tile([P, 1024], BF16, name="bias_row")
-        bias_bc = const.tile([P, 2, 4, P], F32, name="bias_bc")
-        bcol = const.tile([P, 8], F32, name="bcol")
+        bias_all = const.tile([P, 2, 4, P], F32, name="bias_all")
+        bias_col = const.tile([P, 8], F32, name="bias_col")
         w_sb = [const.tile([P, 4, 512], BF16, name="w_sb%d" % kv) for kv in range(2)]
         w_codes = [const.tile([P, 512], U32, name="w_codes%d" % kv, align_bytes=64) for kv in range(2)]
         w_scales = [const.tile([P, 512], U8, name="w_scales%d" % kv, align_bytes=64) for kv in range(2)]
         x_sb = [const.tile([P, 2, 8, 512], BF16, name="x_sb%d" % g) for g in range(FAMILIES)]
-        x_codes2 = const.tile([P, 16, P], U32, name="x_codes2", align_bytes=64)
-        x_scales2 = const.tile([P, 16, P], U8, name="x_scales2", align_bytes=64)
-        x_codes01 = const.tile([P, 16, 2, P], U32, name="x_codes01", align_bytes=64)
-        x_scales01 = const.tile([P, 16, 2, P], U8, name="x_scales01", align_bytes=64)
-
-        def token_set(g, s):
-            if g == 2:
-                return x_codes2[:, s, :], x_scales2[:, s, :]
-            return x_codes01[:, s, g, :], x_scales01[:, s, g, :]
-
-        red = const.tile([P, 8, 48], F32, name="red")
+        x_codes0 = const.tile([P, 16, P], U32, name="x_codes0", align_bytes=64)
+        x_scales0 = const.tile([P, 16, P], U8, name="x_scales0", align_bytes=64)
+        x_codes12 = const.tile([P, 16, 2, P], U32, name="x_codes12", align_bytes=64)
+        x_scales12 = const.tile([P, 16, 2, P], U8, name="x_scales12", align_bytes=64)
+        sums = const.tile([P, 8, 48], F32, name="sums")
         mean_sb = const.tile([P, 8, 48], F32, name="mean_sb")
-        mt_sb = const.tile([P, 3, P], F32, name="mt_sb")
-
-        state = {"clock": 0, "pending": []}
-
-        def later(lag, fn):
-            state["pending"].append((state["clock"] + lag, fn))
-
-        def tick():
-            state["clock"] += 1
-            due = [x for x in state["pending"] if x[0] <= state["clock"]]
-            state["pending"] = [x for x in state["pending"] if x[0] > state["clock"]]
-            for x in due:
-                x[1]()
+        mean_rows = const.tile([P, 3, P], F32, name="mean_rows")
 
         for kv in range(2):
             nc.scalar.dma_start(out=bias_in[0:1, 512 * kv : 512 * kv + 512], in_=b_dram[kv])
+        nc.sync.dma_start(out=w_sb[0][:], in_=w_dram[0])
+        for g, first, end in ((0, 0, 2), (0, 2, 4), (0, 4, 6), (0, 6, 8)):
+            nc.sync.dma_start(out=x_sb[g][:, :, first:end, :], in_=x_dram[g][:, :, first:end, :])
+        nc.sync.dma_start(out=w_sb[1][:], in_=w_dram[1])
+        for g, first, end in ((1, 0, 4), (1, 4, 8), (2, 0, 4), (2, 4, 8)):
+            nc.sync.dma_start(out=x_sb[g][:, :, first:end, :], in_=x_dram[g][:, :, first:end, :])
+
         nc.vector.memset(bias_row[:], 0.0)
         nc.vector.memset(ones[:], 1.0)
         make_identity(nc, ident_f[:])
         make_identity(nc, ident_b[:])
 
-        def load_x(g, a, b):
-            nc.sync.dma_start(out=x_sb[g][:, :, a:b, :], in_=hs[g][:, :, a:b, :])
+        def transpose_and_regroup(rows, tag, slots, copies):
+            grouped = stage.tile([P, 2048], BF16, name="grouped", align_bytes=64)
+            words = grouped[:].bitcast(F32).rearrange("q (s t u) -> q s t u", s=4, u=2)
+            banks = []
+            for b in range(2):
+                bank = psum.tile([P, 2, 2, P], F32, name="bank_" + tag, tag=tag, bufs=slots)
+                for s in range(2):
+                    for u in range(2):
+                        nc.tensor.transpose(bank[:, s, u, :], rows[2 * b + s][:, P * u : P * u + P], ident_f[:])
+                banks.append(bank)
+            for b in range(2):
+                copies[b](out=words[:, 2 * b : 2 * b + 2], in_=banks[b][:].rearrange("q s u t -> q s t u"))
+            return grouped
 
-        nc.sync.dma_start(out=w_sb[0][:], in_=w_dram[0])
-        load_x(0, 0, 2)
-        load_x(0, 2, 4)
-        load_x(0, 4, 8)
-        nc.sync.dma_start(out=w_sb[1][:], in_=w_dram[1])
-        load_x(1, 0, 4)
-        load_x(1, 4, 8)
-        load_x(2, 0, 4)
-        load_x(2, 4, 8)
-
-        def bias_everywhere(kv, tag, lag):
-            bb_ps = psum.tile([P, 512], F32, name="bb_ps", tag=tag, bufs=(4 if tag == "y" else 2))
-            nc.tensor.matmul(
-                out=bb_ps[:], lhsT=ones[:], rhs=bias_row[:, 512 * kv : 512 * kv + 512], start=True, stop=True
-            )
-            copy_out = nc.vector.tensor_copy if kv == 0 else nc.scalar.copy
-            later(lag, lambda: copy_out(out=bias_bc[:, kv].rearrange("p h d -> p (h d)"), in_=bb_ps[:]))
-
-        def bias_columns():
-            bc_ps = psum.tile([P, 8, P], BF16, name="bc_ps", tag="y", bufs=4)
-            for fb in range(8):
-                nc.tensor.transpose(bc_ps[:, fb, :], bias_row[:, P * fb : P * fb + P], ident_b[:])
-            later(2, lambda: nc.vector.tensor_copy(out=bcol[:], in_=bc_ps[:, :, 0]))
-
-        def transposed_bank(words, tag):
-            bank = psum.tile([P, 2, 2, P], F32, name="bank_" + tag, tag=tag, bufs=(4 if tag == "y" else 2))
-            for s in range(2):
-                for u in range(2):
-                    nc.tensor.transpose(bank[:, s, u, :], words[s][:, P * u : P * u + P], ident_f[:])
-            return bank
-
-        def regroup(engine_copy, grouped, b, bank):
-            view = grouped[:].bitcast(F32).rearrange("q (s t u) -> q s t u", s=4, u=2)
-            engine_copy(out=view[:, 2 * b : 2 * b + 2], in_=bank[:].rearrange("q s u t -> q s t u"))
-
-        def prepare_w(kv, lag):
+        def transpose_w(kv, copies):
             words = w_sb[kv][:].bitcast(F32)
-            grouped = stage.tile([P, 2048], BF16, name="grouped", align_bytes=64)
-            banks = [transposed_bank([words[:, 2 * b + s, :] for s in range(2)], "y") for b in range(2)]
-            regroup(nc.vector.tensor_copy if kv == 0 else nc.scalar.copy, grouped, 0, banks[0])
-            regroup(nc.scalar.copy, grouped, 1, banks[1])
-            if kv == 0:
-                nc.vector.tensor_copy(out=bias_row[0:1, :], in_=bias_in[:])
-            later(
-                lag,
-                lambda: nc.vector.quantize_mx(
-                    out=w_codes[kv][:].bitcast(FP8X4), scales=w_scales[kv][:], in_=grouped[:]
-                ),
-            )
+            return transpose_and_regroup([words[:, ob, :] for ob in range(4)], "y", 4, copies)
 
-        def prepare_x(g, rr, lag, share):
+        def quantise_w(kv, grouped):
+            nc.vector.quantize_mx(out=w_codes[kv][:].bitcast(FP8X4), scales=w_scales[kv][:], in_=grouped[:])
+
+        def transpose_x(g, run, copies):
             words = x_sb[g][:].bitcast(F32)
-            grouped = stage.tile([P, 2048], BF16, name="grouped", align_bytes=64)
-            banks = [transposed_bank([words[:, jh, 2 * rr + b, :] for jh in range(2)], "t") for b in range(2)]
-            regroup(nc.scalar.copy, grouped, 0, banks[0])
-            regroup(nc.vector.tensor_copy if share else nc.scalar.copy, grouped, 1, banks[1])
+            return transpose_and_regroup([words[:, s % 2, 2 * run + s // 2, :] for s in range(4)], "t", 2, copies)
 
-            def quantise():
-                if g == 2:
-                    sets = slice(4 * rr, 4 * rr + 4)
+        def token_set(g, s):
+            if g == 0:
+                return x_codes0[:, s, :], x_scales0[:, s, :]
+            return x_codes12[:, s, g - 1, :], x_scales12[:, s, g - 1, :]
+
+        def quantise_x(g, run, grouped):
+            if g == 0:
+                sets = slice(4 * run, 4 * run + 4)
+                nc.vector.quantize_mx(
+                    out=x_codes0[:, sets, :].rearrange("q s t -> q (s t)").bitcast(FP8X4),
+                    scales=x_scales0[:, sets, :].rearrange("q s t -> q (s t)"),
+                    in_=grouped[:],
+                )
+            else:
+                for s in range(4):
+                    codes, scales = token_set(g, 4 * run + s)
                     nc.vector.quantize_mx(
-                        out=x_codes2[:, sets, :].rearrange("q s t -> q (s t)").bitcast(FP8X4),
-                        scales=x_scales2[:, sets, :].rearrange("q s t -> q (s t)"),
-                        in_=grouped[:],
+                        out=codes.bitcast(FP8X4), scales=scales, in_=grouped[:, 512 * s : 512 * s + 512]
                     )
-                else:
-                    for s in range(4):
-                        codes, scales = token_set(g, 4 * rr + s)
-                        nc.vector.quantize_mx(
-                            out=codes.bitcast(FP8X4), scales=scales, in_=grouped[:, 512 * s : 512 * s + 512]
-                        )
 
-            later(lag, quantise)
+        def bias_to_all_partitions(kv, tag, slots, copy):
+            product = psum.tile([P, 512], F32, name="product", tag=tag, bufs=slots)
+            nc.tensor.matmul(
+                out=product[:], lhsT=ones[:], rhs=bias_row[:, 512 * kv : 512 * kv + 512], start=True, stop=True
+            )
+            copy(out=bias_all[:, kv].rearrange("p h d -> p (h d)"), in_=product[:])
 
-        units = {}
+        def bias_to_columns():
+            flipped = psum.tile([P, 8, P], BF16, name="flipped", tag="y", bufs=4)
+            for fb in range(8):
+                nc.tensor.transpose(flipped[:, fb, :], bias_row[:, P * fb : P * fb + P], ident_b[:])
+            nc.scalar.copy(out=bias_col[:], in_=flipped[:, :, 0])
 
-        def y_bank(g, kv, hh, i):
-            key = (g, kv, hh)
-            if key not in units:
-                units[key] = ypool.tile([P, 2, 2, 8, P], F32, name="yb")
-            yb = units[key]
-            y_ps = psum.tile([P, 2, 256], F32, name="y_ps", tag="y", bufs=4)
+        def project(g, kv, hh, i):
+            bank = psum.tile([P, 2, 256], F32, name="y_bank", tag="y", bufs=4)
             feats = slice(256 * hh, 256 * hh + 256)
             for jh in range(2):
                 codes, scales = token_set(g, 2 * i + jh)
                 nc.tensor.matmul_mx(
-                    out=y_ps[:, jh, :],
+                    out=bank[:, jh, :],
                     lhsT=codes.bitcast(FP8X4),
                     lhsT_scale=scales,
                     rhs=w_codes[kv][:, feats].bitcast(FP8X4),
@@ -185,152 +145,136 @@ def tile_chunkedattention_pb_t_kernel(
                     start=True,
                     stop=True,
                 )
-            dst = yb[:, :, :, i, :].rearrange("p h jh d -> p jh h d")
-            src = y_ps[:].rearrange("p jh (h d) -> p jh h d", h=2)
-            bias = bias_bc[:, kv, 2 * hh : 2 * hh + 2, :].unsqueeze(1).to_broadcast([P, 2, 2, P])
-            if i in SG_OF_UNIT[4 * g + 2 * kv + hh]:
+            return bank
+
+        def add_bias(bank, unit, kv, hh, i, by_vector):
+            dst = unit[:, :, :, i, :].rearrange("p h jh d -> p jh h d")
+            src = bank[:].rearrange("p jh (h d) -> p jh h d", h=2)
+            bias = bias_all[:, kv, 2 * hh : 2 * hh + 2, :].unsqueeze(1).to_broadcast([P, 2, 2, P])
+            if by_vector:
+                nc.vector.tensor_tensor(out=dst, in0=src, in1=bias, op=ADD)
+            else:
                 nc.scalar.copy(out=dst, in_=src)
                 nc.gpsimd.tensor_tensor(out=dst, in0=dst, in1=bias, op=ADD)
-            else:
-                nc.vector.tensor_tensor(out=dst, in0=src, in1=bias, op=ADD)
 
-        def store_unit(g, kv, hh):
-            yb = units[(g, kv, hh)]
-            nc.sync.dma_start(
-                out=y_dram[kv][g][:, 2 * hh : 2 * hh + 2, :], in_=yb[:].rearrange("p h jh i d -> p h (jh i d)")
+        def sum_pass(group, pair, fb, n):
+            feats = slice(P * (fb % 4), P * (fb % 4) + P)
+            if pair:
+                codes, scales = x_codes12[:, n, :, :], x_scales12[:, n, :, :]
+            else:
+                codes, scales = x_codes0[:, 2 * n : 2 * n + 2, :], x_scales0[:, 2 * n : 2 * n + 2, :]
+            nc.tensor.matmul_mx(
+                out=group[:],
+                lhsT=w_codes[fb // 4][:, feats].bitcast(FP8X4),
+                lhsT_scale=w_scales[fb // 4][:, feats],
+                rhs=codes.rearrange("q a t -> q (a t)").bitcast(FP8X4),
+                rhs_scale=scales.rearrange("q a t -> q (a t)"),
+                start=(n == 0),
+                stop=(n == (15 if pair else 7)),
             )
 
-        def store_piece(g, kv, hh, a, b):
-            yb = units[(g, kv, hh)]
-            for h in range(2):
-                nc.sync.dma_start(
-                    out=y_dram[kv][g][:, 2 * hh + h, :].rearrange("p (jh i d) -> p jh i d", jh=2, i=8)[:, :, a:b, :],
-                    in_=yb[:, h, :, a:b, :],
+        def reduce_group(group, pair, fb):
+            if pair:
+                nc.vector.tensor_reduce(
+                    out=sums[:, fb, 16:48], in_=group[:].rearrange("d (c s) -> d c s", s=8), axis=AXIS.X, op=ADD
+                )
+                nc.scalar.activation(
+                    out=mean_sb[:, fb, :],
+                    in_=sums[:, fb, :],
+                    func=IDENTITY,
+                    bias=bias_col[:, fb : fb + 1],
+                    scale=1.0 / 128.0,
+                )
+            else:
+                nc.vector.tensor_reduce(
+                    out=sums[:, fb, 0:16],
+                    in_=group[:].rearrange("d (jh c s) -> d c jh s", jh=2, s=8),
+                    axis=AXIS.XY,
+                    op=ADD,
                 )
 
-        m_tiles = {}
-
-        def m_pass(g, fb, i):
-            kv, h = fb // 4, fb % 4
-            last = 7 if g == 2 else 15
-            if i == 0:
-                m_tiles[(g, fb)] = psum.tile([P, 256], F32, name="m_ps", tag="m")
-            m_ps = m_tiles[(g, fb)]
-            feats = slice(P * h, P * h + P)
-            if g == 2:
-                codes = x_codes2[:, 2 * i : 2 * i + 2, :].rearrange("q s t -> q (s t)")
-                scales = x_scales2[:, 2 * i : 2 * i + 2, :].rearrange("q s t -> q (s t)")
-            else:
-                codes = x_codes01[:, i, :, :].rearrange("q g t -> q (g t)")
-                scales = x_scales01[:, i, :, :].rearrange("q g t -> q (g t)")
-            nc.tensor.matmul_mx(
-                out=m_ps[:],
-                lhsT=w_codes[kv][:, feats].bitcast(FP8X4),
-                lhsT_scale=w_scales[kv][:, feats],
-                rhs=codes.bitcast(FP8X4),
-                rhs_scale=scales,
-                start=(i == 0),
-                stop=(i == last),
-            )
-            if i == last:
-
-                def reduce_block():
-                    if g == 0:
-                        nc.vector.tensor_reduce(
-                            out=red[:, fb, 0:32],
-                            in_=m_ps[:].rearrange("d (c s) -> d c s", s=8),
-                            axis=mybir.AxisListType.X,
-                            op=ADD,
-                        )
-                    else:
-                        nc.vector.tensor_reduce(
-                            out=red[:, fb, 32:48],
-                            in_=m_ps[:].rearrange("d (jh c s) -> d c jh s", jh=2, s=8),
-                            axis=mybir.AxisListType.XY,
-                            op=ADD,
-                        )
-                        nc.scalar.activation(
-                            out=mean_sb[:, fb, :],
-                            in_=red[:, fb, :],
-                            func=mybir.ActivationFunctionType.Identity,
-                            bias=bcol[:, fb : fb + 1],
-                            scale=1.0 / 128.0,
-                        )
-
-                later(R_LAG, reduce_block)
-
-        def finish_means():
-            mt_ps = psum.tile([P, 3, P], F32, name="mt_ps", tag="t")
-            flat = mean_sb[:].rearrange("d fb c -> d (fb c)")
+        def store_means():
+            flipped = psum.tile([P, 3, P], F32, name="mean_flipped", tag="t")
+            columns = mean_sb[:].rearrange("d fb c -> d (fb c)")
             for b in range(3):
-                nc.tensor.transpose(mt_ps[:, b, :], flat[:, P * b : P * b + P], ident_f[:])
-            nc.scalar.copy(out=mt_sb[:], in_=mt_ps[:])
-            nc.sync.dma_start(out=mean_dram[0][0:128, :], in_=mt_sb[:, 0, :])
-            nc.sync.dma_start(out=mean_dram[0][128:192, :], in_=mt_sb[0:64, 1, :])
-            nc.sync.dma_start(out=mean_dram[1][0:64, :], in_=mt_sb[64:128, 1, :])
-            nc.sync.dma_start(out=mean_dram[1][64:192, :], in_=mt_sb[:, 2, :])
+                nc.tensor.transpose(flipped[:, b, :], columns[:, P * b : P * b + P], ident_f[:])
+            nc.scalar.copy(out=mean_rows[:], in_=flipped[:])
+            nc.sync.dma_start(out=mean_dram[0][0:128, :], in_=mean_rows[:, 0, :])
+            nc.sync.dma_start(out=mean_dram[0][128:192, :], in_=mean_rows[0:64, 1, :])
+            nc.sync.dma_start(out=mean_dram[1][0:64, :], in_=mean_rows[64:128, 1, :])
+            nc.sync.dma_start(out=mean_dram[1][64:192, :], in_=mean_rows[:, 2, :])
 
-        def first_work(rr):
-            for i in (2 * rr, 2 * rr + 1):
-                y_bank(0, 0, 0, i)
-                tick()
+        shared = (nc.vector.tensor_copy, nc.scalar.copy)
+        scalar_only = (nc.scalar.copy, nc.scalar.copy)
+        grouped = transpose_w(0, shared)
+        nc.vector.tensor_copy(out=bias_row[0:1, :], in_=bias_in[:])
+        quantise_w(0, grouped)
+        grouped = transpose_x(0, 0, shared)
+        quantise_x(0, 0, grouped)
+        bias_to_all_partitions(0, "m", 2, nc.vector.tensor_copy)
+        grouped = transpose_x(0, 1, scalar_only)
+        quantise_x(0, 1, grouped)
 
-        def second_unit(a, b):
-            for i in range(a, b):
-                y_bank(0, 0, 1, i)
-                tick()
-
-        prepare_w(0, 1)
-        tick()
-        prepare_x(0, 0, 1, True)
-        bias_everywhere(0, "m", 1)
-        tick()
-        prepare_x(0, 1, 2, False)
-        tick()
-        first_work(0)
-        prepare_x(0, 2, 3, False)
-        tick()
-        first_work(1)
-        prepare_x(0, 3, 4, False)
-        tick()
-        second_unit(0, 4)
-        first_work(2)
-        first_work(3)
-        store_unit(0, 0, 0)
-        prepare_w(1, 3)
-        bias_everywhere(1, "y", 2)
-        bias_columns()
-        tick()
-        second_unit(4, 6)
-        prepare_x(1, 0, Q_LAG, False)
-        tick()
-        second_unit(6, 8)
-        store_unit(0, 0, 1)
-
-        y_list = [
-            (g, kv, hh, i)
+        halves = [(0, 0, 0, 0), (0, 0, 1, 0), (0, 0, 0, 1), (0, 0, 1, 1)] + [
+            (g, kv, hh, half)
             for g in range(FAMILIES)
             for kv in range(2)
             for hh in range(2)
-            for i in range(8)
+            for half in range(2)
             if (g, kv) != (0, 0)
         ]
-        m_list = [(0, fb, i) for fb in range(8) for i in range(16)] + [(2, fb, i) for fb in range(8) for i in range(8)]
-        m_next = 0
-        for n, (g, kv, hh, i) in enumerate(y_list):
-            if n in T_AT:
-                prepare_x(T_AT[n][0], T_AT[n][1], Q_LAG, False)
-                tick()
-            y_bank(g, kv, hh, i)
-            m_upto = min(192, max(0, 192 * (n + 1 - M_START) // (M_END - M_START)))
-            for m in m_list[m_next:m_upto]:
-                m_pass(m[0], m[1], m[2])
-            m_next = m_upto
-            tick()
-            if n == M_END + 3:
-                finish_means()
-            if (g, kv, hh) == (2, 1, 1):
-                if i in (3, 5, 7):
-                    store_piece(g, kv, hh, {3: 0, 5: 4, 7: 6}[i], i + 1)
-            elif i == 7:
-                store_unit(g, kv, hh)
+        preparations = [(0, 2), (0, 3), "wv"] + [(g, run) for g in (1, 2) for run in range(4)]
+        passes = [(False, fb, n) for fb in range(8) for n in range(8)]
+        passes += [(True, fb, n) for fb in range(8) for n in range(16)]
+        next_pass = 0
+        units = {}
+        group = None
+        closed = None
+        for r in range(ROUNDS):
+            g, kv, hh, half = halves[r]
+            if half == 0:
+                units[(g, kv, hh)] = ypool.tile([P, 2, 2, 8, P], F32, name="unit")
+            unit = units[(g, kv, hh)]
+            prep = preparations[r] if r < len(preparations) else None
+            if prep == "wv":
+                grouped = transpose_w(1, scalar_only)
+                bias_to_all_partitions(1, "y", 4, nc.scalar.copy)
+                bias_to_columns()
+            elif prep is not None:
+                grouped = transpose_x(prep[0], prep[1], scalar_only)
+            if r < 2 or r == ROUNDS - 1:
+                per_bank = 0
+            else:
+                per_bank = 3 if r in DENSE_ROUNDS else 2
+            for b in range(4):
+                i = 4 * half + b
+                bank = project(g, kv, hh, i)
+                closing = None
+                for n in range(per_bank):
+                    pair, fb, number = passes[next_pass]
+                    next_pass += 1
+                    if number == 0:
+                        group = psum.tile([P, 256], F32, name="group", tag="m")
+                    sum_pass(group, pair, fb, number)
+                    if number == (15 if pair else 7):
+                        closing = (group, pair, fb)
+                add_bias(bank, unit, kv, hh, i, b != 2 or r == ROUNDS - 1)
+                if closed is not None:
+                    reduce_group(closed[0], closed[1], closed[2])
+                closed = closing
+                if r == ROUNDS - 1 and b == 1:
+                    store_means()
+                if b == 1 and prep == "wv":
+                    quantise_w(1, grouped)
+                elif b == 1 and prep is not None:
+                    quantise_x(prep[0], prep[1], grouped)
+            if r >= ROUNDS - 4:
+                for h in range(2):
+                    head = y_dram[kv][g][:, 2 * hh + h, :].rearrange("p (jh i d) -> p jh i d", jh=2, i=8)
+                    nc.sync.dma_start(
+                        out=head[:, :, 4 * half : 4 * half + 4, :], in_=unit[:, h, :, 4 * half : 4 * half + 4, :]
+                    )
+            elif half == 1:
+                nc.sync.dma_start(
+                    out=y_dram[kv][g][:, 2 * hh : 2 * hh + 2, :], in_=unit[:].rearrange("p h jh i d -> p h (jh i d)")
+                )

@@ -17,7 +17,6 @@ IDENTITY = mybir.ActivationFunctionType.Identity
 P = 128
 FAMILIES = 3
 ROUNDS = 24
-DENSE_ROUNDS = range(11, 17)
 
 
 def tile_chunkedattention_pb_t_kernel(
@@ -44,6 +43,8 @@ def tile_chunkedattention_pb_t_kernel(
         ident_b = const.tile([P, P], BF16, name="ident_b")
         ones = const.tile([P, P], BF16, name="ones")
         bias_in = const.tile([1, 1024], BF16, name="bias_in")
+        blocks_in = const.tile([8, P], BF16, name="blocks_in")
+        bias_blocks = const.tile([P, P], BF16, name="bias_blocks")
         bias_row = const.tile([P, 1024], BF16, name="bias_row")
         bias_all = const.tile([P, 2, 4, P], F32, name="bias_all")
         bias_col = const.tile([P, 8], F32, name="bias_col")
@@ -51,16 +52,15 @@ def tile_chunkedattention_pb_t_kernel(
         w_codes = [const.tile([P, 512], U32, name="w_codes%d" % kv, align_bytes=64) for kv in range(2)]
         w_scales = [const.tile([P, 512], U8, name="w_scales%d" % kv, align_bytes=64) for kv in range(2)]
         x_sb = [const.tile([P, 2, 8, 512], BF16, name="x_sb%d" % g) for g in range(FAMILIES)]
-        x_codes0 = const.tile([P, 16, P], U32, name="x_codes0", align_bytes=64)
-        x_scales0 = const.tile([P, 16, P], U8, name="x_scales0", align_bytes=64)
-        x_codes12 = const.tile([P, 16, 2, P], U32, name="x_codes12", align_bytes=64)
-        x_scales12 = const.tile([P, 16, 2, P], U8, name="x_scales12", align_bytes=64)
+        x_codes = [const.tile([P, 16, P], U32, name="x_codes%d" % g, align_bytes=64) for g in range(FAMILIES)]
+        x_scales = [const.tile([P, 16, P], U8, name="x_scales%d" % g, align_bytes=64) for g in range(FAMILIES)]
         sums = const.tile([P, 8, 48], F32, name="sums")
         mean_sb = const.tile([P, 8, 48], F32, name="mean_sb")
         mean_rows = const.tile([P, 3, P], F32, name="mean_rows")
 
         for kv in range(2):
             nc.scalar.dma_start(out=bias_in[0:1, 512 * kv : 512 * kv + 512], in_=b_dram[kv])
+            nc.scalar.dma_start(out=blocks_in[4 * kv : 4 * kv + 4, :], in_=b_dram[kv].rearrange("o (h d) -> (o h) d", h=4))
         nc.sync.dma_start(out=w_sb[0][:], in_=w_dram[0])
         for g, first, end in ((0, 0, 2), (0, 2, 4), (0, 4, 6), (0, 6, 8)):
             nc.sync.dma_start(out=x_sb[g][:, :, first:end, :], in_=x_dram[g][:, :, first:end, :])
@@ -69,6 +69,7 @@ def tile_chunkedattention_pb_t_kernel(
             nc.sync.dma_start(out=x_sb[g][:, :, first:end, :], in_=x_dram[g][:, :, first:end, :])
 
         nc.vector.memset(bias_row[:], 0.0)
+        nc.vector.memset(bias_blocks[:], 0.0)
         nc.vector.memset(ones[:], 1.0)
         make_identity(nc, ident_f[:])
         make_identity(nc, ident_b[:])
@@ -87,9 +88,9 @@ def tile_chunkedattention_pb_t_kernel(
                 copies[b](out=words[:, 2 * b : 2 * b + 2], in_=banks[b][:].rearrange("q s u t -> q s t u"))
             return grouped
 
-        def transpose_w(kv, copies):
+        def transpose_w(kv, tag, slots, copies):
             words = w_sb[kv][:].bitcast(F32)
-            return transpose_and_regroup([words[:, ob, :] for ob in range(4)], "y", 4, copies)
+            return transpose_and_regroup([words[:, ob, :] for ob in range(4)], tag, slots, copies)
 
         def quantise_w(kv, grouped):
             nc.vector.quantize_mx(out=w_codes[kv][:].bitcast(FP8X4), scales=w_scales[kv][:], in_=grouped[:])
@@ -98,25 +99,13 @@ def tile_chunkedattention_pb_t_kernel(
             words = x_sb[g][:].bitcast(F32)
             return transpose_and_regroup([words[:, s % 2, 2 * run + s // 2, :] for s in range(4)], "t", 2, copies)
 
-        def token_set(g, s):
-            if g == 0:
-                return x_codes0[:, s, :], x_scales0[:, s, :]
-            return x_codes12[:, s, g - 1, :], x_scales12[:, s, g - 1, :]
-
         def quantise_x(g, run, grouped):
-            if g == 0:
-                sets = slice(4 * run, 4 * run + 4)
-                nc.vector.quantize_mx(
-                    out=x_codes0[:, sets, :].rearrange("q s t -> q (s t)").bitcast(FP8X4),
-                    scales=x_scales0[:, sets, :].rearrange("q s t -> q (s t)"),
-                    in_=grouped[:],
-                )
-            else:
-                for s in range(4):
-                    codes, scales = token_set(g, 4 * run + s)
-                    nc.vector.quantize_mx(
-                        out=codes.bitcast(FP8X4), scales=scales, in_=grouped[:, 512 * s : 512 * s + 512]
-                    )
+            sets = slice(4 * run, 4 * run + 4)
+            nc.vector.quantize_mx(
+                out=x_codes[g][:, sets, :].rearrange("q s t -> q (s t)").bitcast(FP8X4),
+                scales=x_scales[g][:, sets, :].rearrange("q s t -> q (s t)"),
+                in_=grouped[:],
+            )
 
         def bias_to_all_partitions(kv, tag, slots, copy):
             product = psum.tile([P, 512], F32, name="product", tag=tag, bufs=slots)
@@ -126,20 +115,18 @@ def tile_chunkedattention_pb_t_kernel(
             copy(out=bias_all[:, kv].rearrange("p h d -> p (h d)"), in_=product[:])
 
         def bias_to_columns():
-            flipped = psum.tile([P, 8, P], BF16, name="flipped", tag="y", bufs=4)
-            for fb in range(8):
-                nc.tensor.transpose(flipped[:, fb, :], bias_row[:, P * fb : P * fb + P], ident_b[:])
-            nc.scalar.copy(out=bias_col[:], in_=flipped[:, :, 0])
+            flipped = psum.tile([P, P], BF16, name="flipped", tag="y", bufs=4)
+            nc.tensor.transpose(flipped[:], bias_blocks[:], ident_b[:])
+            nc.scalar.copy(out=bias_col[:], in_=flipped[:, 0:8])
 
         def project(g, kv, hh, i):
             bank = psum.tile([P, 2, 256], F32, name="y_bank", tag="y", bufs=4)
             feats = slice(256 * hh, 256 * hh + 256)
             for jh in range(2):
-                codes, scales = token_set(g, 2 * i + jh)
                 nc.tensor.matmul_mx(
                     out=bank[:, jh, :],
-                    lhsT=codes.bitcast(FP8X4),
-                    lhsT_scale=scales,
+                    lhsT=x_codes[g][:, 2 * i + jh, :].bitcast(FP8X4),
+                    lhsT_scale=x_scales[g][:, 2 * i + jh, :],
                     rhs=w_codes[kv][:, feats].bitcast(FP8X4),
                     rhs_scale=w_scales[kv][:, feats],
                     start=True,
@@ -157,27 +144,28 @@ def tile_chunkedattention_pb_t_kernel(
                 nc.scalar.copy(out=dst, in_=src)
                 nc.gpsimd.tensor_tensor(out=dst, in0=dst, in1=bias, op=ADD)
 
-        def sum_pass(group, pair, fb, n):
+        def sum_pass(g, fb, n):
+            if n == 0:
+                groups[(g, fb)] = psum.tile([P, 256], F32, name="group", tag="m")
             feats = slice(P * (fb % 4), P * (fb % 4) + P)
-            if pair:
-                codes, scales = x_codes12[:, n, :, :], x_scales12[:, n, :, :]
-            else:
-                codes, scales = x_codes0[:, 2 * n : 2 * n + 2, :], x_scales0[:, 2 * n : 2 * n + 2, :]
             nc.tensor.matmul_mx(
-                out=group[:],
+                out=groups[(g, fb)][:],
                 lhsT=w_codes[fb // 4][:, feats].bitcast(FP8X4),
                 lhsT_scale=w_scales[fb // 4][:, feats],
-                rhs=codes.rearrange("q a t -> q (a t)").bitcast(FP8X4),
-                rhs_scale=scales.rearrange("q a t -> q (a t)"),
+                rhs=x_codes[g][:, 2 * n : 2 * n + 2, :].rearrange("q s t -> q (s t)").bitcast(FP8X4),
+                rhs_scale=x_scales[g][:, 2 * n : 2 * n + 2, :].rearrange("q s t -> q (s t)"),
                 start=(n == 0),
-                stop=(n == (15 if pair else 7)),
+                stop=(n == 7),
             )
 
-        def reduce_group(group, pair, fb):
-            if pair:
-                nc.vector.tensor_reduce(
-                    out=sums[:, fb, 16:48], in_=group[:].rearrange("d (c s) -> d c s", s=8), axis=AXIS.X, op=ADD
-                )
+        def reduce_group(g, fb):
+            nc.vector.tensor_reduce(
+                out=sums[:, fb, 16 * g : 16 * g + 16],
+                in_=groups[(g, fb)][:].rearrange("d (jh c s) -> d c jh s", jh=2, s=8),
+                axis=AXIS.XY,
+                op=ADD,
+            )
+            if g == FAMILIES - 1:
                 nc.scalar.activation(
                     out=mean_sb[:, fb, :],
                     in_=sums[:, fb, :],
@@ -185,29 +173,19 @@ def tile_chunkedattention_pb_t_kernel(
                     bias=bias_col[:, fb : fb + 1],
                     scale=1.0 / 128.0,
                 )
-            else:
-                nc.vector.tensor_reduce(
-                    out=sums[:, fb, 0:16],
-                    in_=group[:].rearrange("d (jh c s) -> d c jh s", jh=2, s=8),
-                    axis=AXIS.XY,
-                    op=ADD,
-                )
 
-        def store_means():
+        def flip_means(first, end):
             flipped = psum.tile([P, 3, P], F32, name="mean_flipped", tag="t")
             columns = mean_sb[:].rearrange("d fb c -> d (fb c)")
-            for b in range(3):
+            for b in range(first, end):
                 nc.tensor.transpose(flipped[:, b, :], columns[:, P * b : P * b + P], ident_f[:])
-            nc.scalar.copy(out=mean_rows[:], in_=flipped[:])
-            nc.sync.dma_start(out=mean_dram[0][0:128, :], in_=mean_rows[:, 0, :])
-            nc.sync.dma_start(out=mean_dram[0][128:192, :], in_=mean_rows[0:64, 1, :])
-            nc.sync.dma_start(out=mean_dram[1][0:64, :], in_=mean_rows[64:128, 1, :])
-            nc.sync.dma_start(out=mean_dram[1][64:192, :], in_=mean_rows[:, 2, :])
+            nc.scalar.copy(out=mean_rows[:, first:end, :], in_=flipped[:, first:end, :])
 
         shared = (nc.vector.tensor_copy, nc.scalar.copy)
         scalar_only = (nc.scalar.copy, nc.scalar.copy)
-        grouped = transpose_w(0, shared)
+        grouped = transpose_w(0, "y", 4, shared)
         nc.vector.tensor_copy(out=bias_row[0:1, :], in_=bias_in[:])
+        nc.vector.tensor_copy(out=bias_blocks[0:8, :], in_=blocks_in[:])
         quantise_w(0, grouped)
         grouped = transpose_x(0, 0, shared)
         quantise_x(0, 0, grouped)
@@ -223,58 +201,60 @@ def tile_chunkedattention_pb_t_kernel(
             for half in range(2)
             if (g, kv) != (0, 0)
         ]
-        preparations = [(0, 2), (0, 3), "wv"] + [(g, run) for g in (1, 2) for run in range(4)]
-        passes = [(False, fb, n) for fb in range(8) for n in range(8)]
-        passes += [(True, fb, n) for fb in range(8) for n in range(16)]
-        next_pass = 0
+        preparations = {0: (0, 2), 1: (0, 3), 2: "wv", 7: "bias columns"}
+        for g in (1, 2):
+            for run in range(4):
+                preparations[8 * g - 5 + run] = (g, run)
+        stream = [(g, fb, n) for g in range(FAMILIES) for fb in range(8) for n in range(8) if (g, fb) > (0, 1)]
         units = {}
-        group = None
-        closed = None
+        groups = {}
+        closed = []
         for r in range(ROUNDS):
             g, kv, hh, half = halves[r]
             if half == 0:
                 units[(g, kv, hh)] = ypool.tile([P, 2, 2, 8, P], F32, name="unit")
             unit = units[(g, kv, hh)]
-            prep = preparations[r] if r < len(preparations) else None
+            prep = preparations.get(r)
             if prep == "wv":
-                grouped = transpose_w(1, scalar_only)
+                grouped = transpose_w(1, "t", 2, scalar_only)
                 bias_to_all_partitions(1, "y", 4, nc.scalar.copy)
+            elif prep == "bias columns":
                 bias_to_columns()
             elif prep is not None:
                 grouped = transpose_x(prep[0], prep[1], scalar_only)
-            if r < 2 or r == ROUNDS - 1:
-                per_bank = 0
-            else:
-                per_bank = 3 if r in DENSE_ROUNDS else 2
             for b in range(4):
                 i = 4 * half + b
                 bank = project(g, kv, hh, i)
-                closing = None
-                for n in range(per_bank):
-                    pair, fb, number = passes[next_pass]
-                    next_pass += 1
-                    if number == 0:
-                        group = psum.tile([P, 256], F32, name="group", tag="m")
-                    sum_pass(group, pair, fb, number)
-                    if number == (15 if pair else 7):
-                        closing = (group, pair, fb)
+                if (g, kv, hh) == (0, 0, 0):
+                    behind = [(0, 0, i), (0, 1, i)]
+                elif r >= 4:
+                    behind = stream[8 * (r - 4) + 2 * b : 8 * (r - 4) + 2 * b + 2]
+                else:
+                    behind = []
+                for sg, fb, n in behind:
+                    sum_pass(sg, fb, n)
                 add_bias(bank, unit, kv, hh, i, b != 2 or r == ROUNDS - 1)
-                if closed is not None:
-                    reduce_group(closed[0], closed[1], closed[2])
-                closed = closing
-                if r == ROUNDS - 1 and b == 1:
-                    store_means()
+                for sg, fb, n in closed:
+                    reduce_group(sg, fb)
+                closed = [x for x in behind if x[2] == 7]
                 if b == 1 and prep == "wv":
                     quantise_w(1, grouped)
-                elif b == 1 and prep is not None:
+                elif b == 1 and prep is not None and prep != "bias columns":
                     quantise_x(prep[0], prep[1], grouped)
-            if r >= ROUNDS - 4:
-                for h in range(2):
-                    head = y_dram[kv][g][:, 2 * hh + h, :].rearrange("p (jh i d) -> p jh i d", jh=2, i=8)
-                    nc.sync.dma_start(
-                        out=head[:, :, 4 * half : 4 * half + 4, :], in_=unit[:, h, :, 4 * half : 4 * half + 4, :]
-                    )
-            elif half == 1:
+            if half == 1:
                 nc.sync.dma_start(
                     out=y_dram[kv][g][:, 2 * hh : 2 * hh + 2, :], in_=unit[:].rearrange("p h jh i d -> p h (jh i d)")
                 )
+        for sg, fb, n in closed:
+            reduce_group(sg, fb)
+        for sg, fb, n in stream[8 * (ROUNDS - 4) :]:
+            sum_pass(sg, fb, n)
+            if n == 7:
+                reduce_group(sg, fb)
+            if (fb, n) == (6, 7):
+                flip_means(0, 2)
+                nc.sync.dma_start(out=mean_dram[0][0:128, :], in_=mean_rows[:, 0, :])
+                nc.sync.dma_start(out=mean_dram[0][128:192, :], in_=mean_rows[0:64, 1, :])
+                nc.sync.dma_start(out=mean_dram[1][0:64, :], in_=mean_rows[64:128, 1, :])
+        flip_means(2, 3)
+        nc.sync.dma_start(out=mean_dram[1][64:192, :], in_=mean_rows[:, 2, :])

from contextlib import ExitStack

import concourse.mybir as mybir
from concourse.masks import make_identity

FLOPS = 2 * 6144 * 512 * 1024

F32 = mybir.dt.float32
BF16 = mybir.dt.bfloat16
U32 = mybir.dt.uint32
U8 = mybir.dt.uint8
FP8X4 = mybir.dt.float8_e4m3fn_x4
ADD = mybir.AluOpType.add
AXIS = mybir.AxisListType
IDENTITY = mybir.ActivationFunctionType.Identity

P = 128
FAMILIES = 3
ROUNDS = 24


def tile_chunkedattention_pb_t_kernel(
    tc, hidden_states, wk, bk, wv, bv, out_0, out_1, out_2, out_3
):
    nc = tc.nc
    with ExitStack() as ctx:
        const = ctx.enter_context(tc.tile_pool(name="const", bufs=1))
        stage = ctx.enter_context(tc.tile_pool(name="stage", bufs=3))
        ypool = ctx.enter_context(tc.tile_pool(name="ypool", bufs=6))
        psum = ctx.enter_context(tc.psum_pool(name="psum", bufs=2))
        ctx.enter_context(tc.manual_schedule())

        x_dram = hidden_states.rearrange("b (g p jh i) e -> (b g) p jh i e", p=P, jh=2, i=8)
        w_dram = [w.rearrange("(ob p) e -> p ob e", p=P) for w in (wk, wv)]
        b_dram = [b.rearrange("(o n) -> o n", o=1) for b in (bk, bv)]
        y_dram = [
            o.rearrange("b h c t d -> (b h) (c t d)").rearrange("h (g p r) -> g p h r", g=FAMILIES, p=P)
            for o in (out_0, out_1)
        ]
        mean_dram = [o.rearrange("b h c d -> (b h c) d") for o in (out_2, out_3)]

        ident_f = const.tile([P, P], F32, name="ident_f")
        ident_b = const.tile([P, P], BF16, name="ident_b")
        ones = const.tile([P, P], BF16, name="ones")
        bias_in = const.tile([1, 1024], BF16, name="bias_in")
        blocks_in = const.tile([8, P], BF16, name="blocks_in")
        bias_blocks = const.tile([P, P], BF16, name="bias_blocks")
        bias_row = const.tile([P, 1024], BF16, name="bias_row")
        bias_all = const.tile([P, 2, 4, P], F32, name="bias_all")
        bias_col = const.tile([P, 8], F32, name="bias_col")
        w_sb = [const.tile([P, 4, 512], BF16, name="w_sb%d" % kv) for kv in range(2)]
        w_codes = [const.tile([P, 512], U32, name="w_codes%d" % kv, align_bytes=64) for kv in range(2)]
        w_scales = [const.tile([P, 512], U8, name="w_scales%d" % kv, align_bytes=64) for kv in range(2)]
        x_sb = [const.tile([P, 2, 8, 512], BF16, name="x_sb%d" % g) for g in range(FAMILIES)]
        x_codes = [const.tile([P, 16, P], U32, name="x_codes%d" % g, align_bytes=64) for g in range(FAMILIES)]
        x_scales = [const.tile([P, 16, P], U8, name="x_scales%d" % g, align_bytes=64) for g in range(FAMILIES)]
        sums = const.tile([P, 8, 48], F32, name="sums")
        mean_sb = const.tile([P, 8, 48], F32, name="mean_sb")
        mean_rows = const.tile([P, 3, P], F32, name="mean_rows")

        for kv in range(2):
            nc.scalar.dma_start(out=bias_in[0:1, 512 * kv : 512 * kv + 512], in_=b_dram[kv])
            nc.scalar.dma_start(out=blocks_in[4 * kv : 4 * kv + 4, :], in_=b_dram[kv].rearrange("o (h d) -> (o h) d", h=4))
        nc.sync.dma_start(out=w_sb[0][:], in_=w_dram[0])
        for g, first, end in ((0, 0, 2), (0, 2, 4), (0, 4, 6), (0, 6, 8)):
            nc.sync.dma_start(out=x_sb[g][:, :, first:end, :], in_=x_dram[g][:, :, first:end, :])
        nc.sync.dma_start(out=w_sb[1][:], in_=w_dram[1])
        for g, first, end in ((1, 0, 4), (1, 4, 8), (2, 0, 4), (2, 4, 8)):
            nc.sync.dma_start(out=x_sb[g][:, :, first:end, :], in_=x_dram[g][:, :, first:end, :])

        nc.vector.memset(bias_row[:], 0.0)
        nc.vector.memset(bias_blocks[:], 0.0)
        nc.vector.memset(ones[:], 1.0)
        make_identity(nc, ident_f[:])
        make_identity(nc, ident_b[:])

        def transpose_and_regroup(rows, tag, slots, copies):
            grouped = stage.tile([P, 2048], BF16, name="grouped", align_bytes=64)
            words = grouped[:].bitcast(F32).rearrange("q (s t u) -> q s t u", s=4, u=2)
            banks = []
            for b in range(2):
                bank = psum.tile([P, 2, 2, P], F32, name="bank_" + tag, tag=tag, bufs=slots)
                for s in range(2):
                    for u in range(2):
                        nc.tensor.transpose(bank[:, s, u, :], rows[2 * b + s][:, P * u : P * u + P], ident_f[:])
                banks.append(bank)
            for b in range(2):
                copies[b](out=words[:, 2 * b : 2 * b + 2], in_=banks[b][:].rearrange("q s u t -> q s t u"))
            return grouped

        def transpose_w(kv, tag, slots, copies):
            words = w_sb[kv][:].bitcast(F32)
            return transpose_and_regroup([words[:, ob, :] for ob in range(4)], tag, slots, copies)

        def quantise_w(kv, grouped):
            nc.vector.quantize_mx(out=w_codes[kv][:].bitcast(FP8X4), scales=w_scales[kv][:], in_=grouped[:])

        def transpose_x(g, run, copies):
            words = x_sb[g][:].bitcast(F32)
            return transpose_and_regroup([words[:, s % 2, 2 * run + s // 2, :] for s in range(4)], "t", 2, copies)

        def quantise_x(g, run, grouped):
            sets = slice(4 * run, 4 * run + 4)
            nc.vector.quantize_mx(
                out=x_codes[g][:, sets, :].rearrange("q s t -> q (s t)").bitcast(FP8X4),
                scales=x_scales[g][:, sets, :].rearrange("q s t -> q (s t)"),
                in_=grouped[:],
            )

        def bias_to_all_partitions(kv, tag, slots, copy):
            product = psum.tile([P, 512], F32, name="product", tag=tag, bufs=slots)
            nc.tensor.matmul(
                out=product[:], lhsT=ones[:], rhs=bias_row[:, 512 * kv : 512 * kv + 512], start=True, stop=True
            )
            copy(out=bias_all[:, kv].rearrange("p h d -> p (h d)"), in_=product[:])

        def bias_to_columns():
            flipped = psum.tile([P, P], BF16, name="flipped", tag="y", bufs=4)
            nc.tensor.transpose(flipped[:], bias_blocks[:], ident_b[:])
            nc.scalar.copy(out=bias_col[:], in_=flipped[:, 0:8])

        def project(g, kv, hh, i):
            bank = psum.tile([P, 2, 256], F32, name="y_bank", tag="y", bufs=4)
            feats = slice(256 * hh, 256 * hh + 256)
            for jh in range(2):
                nc.tensor.matmul_mx(
                    out=bank[:, jh, :],
                    lhsT=x_codes[g][:, 2 * i + jh, :].bitcast(FP8X4),
                    lhsT_scale=x_scales[g][:, 2 * i + jh, :],
                    rhs=w_codes[kv][:, feats].bitcast(FP8X4),
                    rhs_scale=w_scales[kv][:, feats],
                    start=True,
                    stop=True,
                )
            return bank

        def add_bias(bank, unit, kv, hh, i, by_vector):
            dst = unit[:, :, :, i, :].rearrange("p h jh d -> p jh h d")
            src = bank[:].rearrange("p jh (h d) -> p jh h d", h=2)
            bias = bias_all[:, kv, 2 * hh : 2 * hh + 2, :].unsqueeze(1).to_broadcast([P, 2, 2, P])
            if by_vector:
                nc.vector.tensor_tensor(out=dst, in0=src, in1=bias, op=ADD)
            else:
                nc.scalar.copy(out=dst, in_=src)
                nc.gpsimd.tensor_tensor(out=dst, in0=dst, in1=bias, op=ADD)

        def sum_pass(g, fb, n):
            if n == 0:
                groups[(g, fb)] = psum.tile([P, 256], F32, name="group", tag="m")
            feats = slice(P * (fb % 4), P * (fb % 4) + P)
            nc.tensor.matmul_mx(
                out=groups[(g, fb)][:],
                lhsT=w_codes[fb // 4][:, feats].bitcast(FP8X4),
                lhsT_scale=w_scales[fb // 4][:, feats],
                rhs=x_codes[g][:, 2 * n : 2 * n + 2, :].rearrange("q s t -> q (s t)").bitcast(FP8X4),
                rhs_scale=x_scales[g][:, 2 * n : 2 * n + 2, :].rearrange("q s t -> q (s t)"),
                start=(n == 0),
                stop=(n == 7),
            )

        def reduce_group(g, fb):
            nc.vector.tensor_reduce(
                out=sums[:, fb, 16 * g : 16 * g + 16],
                in_=groups[(g, fb)][:].rearrange("d (jh c s) -> d c jh s", jh=2, s=8),
                axis=AXIS.XY,
                op=ADD,
            )
            if g == FAMILIES - 1:
                nc.scalar.activation(
                    out=mean_sb[:, fb, :],
                    in_=sums[:, fb, :],
                    func=IDENTITY,
                    bias=bias_col[:, fb : fb + 1],
                    scale=1.0 / 128.0,
                )

        def flip_means(first, end):
            flipped = psum.tile([P, 3, P], F32, name="mean_flipped", tag="t")
            columns = mean_sb[:].rearrange("d fb c -> d (fb c)")
            for b in range(first, end):
                nc.tensor.transpose(flipped[:, b, :], columns[:, P * b : P * b + P], ident_f[:])
            nc.scalar.copy(out=mean_rows[:, first:end, :], in_=flipped[:, first:end, :])

        shared = (nc.vector.tensor_copy, nc.scalar.copy)
        scalar_only = (nc.scalar.copy, nc.scalar.copy)
        grouped = transpose_w(0, "y", 4, shared)
        nc.vector.tensor_copy(out=bias_row[0:1, :], in_=bias_in[:])
        nc.vector.tensor_copy(out=bias_blocks[0:8, :], in_=blocks_in[:])
        quantise_w(0, grouped)
        grouped = transpose_x(0, 0, shared)
        quantise_x(0, 0, grouped)
        bias_to_all_partitions(0, "m", 2, nc.vector.tensor_copy)
        grouped = transpose_x(0, 1, scalar_only)
        quantise_x(0, 1, grouped)

        halves = [(0, 0, 0, 0), (0, 0, 1, 0), (0, 0, 0, 1), (0, 0, 1, 1)] + [
            (g, kv, hh, half)
            for g in range(FAMILIES)
            for kv in range(2)
            for hh in range(2)
            for half in range(2)
            if (g, kv) != (0, 0)
        ]
        preparations = {0: (0, 2), 1: (0, 3), 2: "wv", 7: "bias columns"}
        for g in (1, 2):
            for run in range(4):
                preparations[8 * g - 5 + run] = (g, run)
        stream = [(g, fb, n) for g in range(FAMILIES) for fb in range(8) for n in range(8) if (g, fb) > (0, 1)]
        units = {}
        groups = {}
        closed = []
        for r in range(ROUNDS):
            g, kv, hh, half = halves[r]
            if half == 0:
                units[(g, kv, hh)] = ypool.tile([P, 2, 2, 8, P], F32, name="unit")
            unit = units[(g, kv, hh)]
            prep = preparations.get(r)
            if prep == "wv":
                grouped = transpose_w(1, "t", 2, scalar_only)
                bias_to_all_partitions(1, "y", 4, nc.scalar.copy)
            elif prep == "bias columns":
                bias_to_columns()
            elif prep is not None:
                grouped = transpose_x(prep[0], prep[1], scalar_only)
            for b in range(4):
                i = 4 * half + b
                bank = project(g, kv, hh, i)
                if (g, kv, hh) == (0, 0, 0):
                    behind = [(0, 0, i), (0, 1, i)]
                elif r >= 4:
                    behind = stream[8 * (r - 4) + 2 * b : 8 * (r - 4) + 2 * b + 2]
                else:
                    behind = []
                for sg, fb, n in behind:
                    sum_pass(sg, fb, n)
                add_bias(bank, unit, kv, hh, i, b != 2 or r == ROUNDS - 1)
                for sg, fb, n in closed:
                    reduce_group(sg, fb)
                closed = [x for x in behind if x[2] == 7]
                if b == 1 and prep == "wv":
                    quantise_w(1, grouped)
                elif b == 1 and prep is not None and prep != "bias columns":
                    quantise_x(prep[0], prep[1], grouped)
            if half == 1:
                nc.sync.dma_start(
                    out=y_dram[kv][g][:, 2 * hh : 2 * hh + 2, :], in_=unit[:].rearrange("p h jh i d -> p h (jh i d)")
                )
        for sg, fb, n in closed:
            reduce_group(sg, fb)
        for sg, fb, n in stream[8 * (ROUNDS - 4) :]:
            sum_pass(sg, fb, n)
            if n == 7:
                reduce_group(sg, fb)
            if (fb, n) == (6, 7):
                flip_means(0, 2)
                nc.sync.dma_start(out=mean_dram[0][0:128, :], in_=mean_rows[:, 0, :])
                nc.sync.dma_start(out=mean_dram[0][128:192, :], in_=mean_rows[0:64, 1, :])
                nc.sync.dma_start(out=mean_dram[1][0:64, :], in_=mean_rows[64:128, 1, :])
        flip_means(2, 3)
        nc.sync.dma_start(out=mean_dram[1][64:192, :], in_=mean_rows[:, 2, :])
